import numpy as np
import ml_dtypes


def mxq(x, axis, fmt="e4m3"):
    dtype, down = {"e4m3": (ml_dtypes.float8_e4m3fn, 7), "e5m2": (ml_dtypes.float8_e5m2, 14)}[fmt]
    v = np.moveaxis(np.asarray(x, np.float32).astype(ml_dtypes.bfloat16).astype(np.float64), axis, -1)
    blocks = v.reshape(v.shape[:-1] + (-1, 32))
    amax = np.abs(blocks).max(-1, keepdims=True)
    byte = np.maximum(np.where(amax > 0, np.frexp(amax)[1] - 1 + 127, 0) - down, 1)
    scale = np.exp2(byte - 127.0)
    codes = (blocks / scale).astype(np.float32).astype(dtype).astype(np.float64)
    return np.moveaxis((codes * scale).reshape(v.shape), -1, axis)


WIDE = False


def mx_kscale(k):
    if not WIDE:
        return np.ones(k)
    levels = np.array([10, -10, 5, -5, 0])
    a = np.random.permutation(np.resize(levels, k // 512 * 4)).reshape(k // 512, 4)
    idx = np.arange(k)
    return np.exp2(a[idx // 512, idx % 128 // 32])


BF16 = ml_dtypes.bfloat16


def bf(x):
    return np.asarray(x, np.float32).astype(BF16)


def f64(x):
    return np.asarray(x).astype(np.float64)


E2M1 = np.array([0.0, 0.5, 1.0, 1.5, 2.0, 3.0, 4.0, 6.0, -0.0, -0.5, -1.0, -1.5, -2.0, -3.0, -4.0, -6.0])


def pack_weight(w, fmt):
    k, n = w.shape
    w = f64(bf(w)).reshape(k // 32, 32, n)
    amax = np.abs(w).max(1)
    if fmt == "e4m3":
        byte = np.frexp(amax)[1] - 1 + 127 - 7
    else:
        mant, ex = np.frexp(amax / 6.0)
        byte = np.where(mant > 0.5, ex, ex - 1) + 127
    byte = np.clip(np.where(amax > 0, byte, 1), 1, 254)
    scaled = (w * np.exp2(127.0 - byte)[:, None, :]).reshape(k, n).astype(np.float32)
    by_word = np.ascontiguousarray(scaled.reshape(k // 512, 128, 4, n).transpose(0, 1, 3, 2))
    if fmt == "e4m3":
        words = by_word.astype(ml_dtypes.float8_e4m3fn).view(np.uint8)
    else:
        c = by_word.astype(ml_dtypes.float4_e2m1fn).view(np.uint8) & 0xF
        words = c[..., 0::2] | (c[..., 1::2] << 4)
    return np.ascontiguousarray(words), np.ascontiguousarray(byte.astype(np.uint8).reshape(k // 512, 16, n))


def unpack_weight(words, scales, fmt):
    g, p, n, _ = words.shape
    if fmt == "e4m3":
        vals = np.ascontiguousarray(words).view(ml_dtypes.float8_e4m3fn).astype(np.float64)
    else:
        nib = np.empty((g, p, n, 4), np.uint8)
        nib[..., 0::2] = words & 0xF
        nib[..., 1::2] = words >> 4
        vals = E2M1[nib]
    vals = vals * np.repeat(np.exp2(scales.astype(np.float64) - 127.0), 8, axis=1)[..., None]
    return vals.transpose(0, 1, 3, 2).reshape(g * 512, n)

def pack4(w):
    words, scales = pack_weight(w, "e2m1")
    return words.reshape(words.shape[0], 128, -1), scales


def unpack4(words, scales):
    return unpack_weight(words.reshape(words.shape[0], 128, -1, 2), scales, "e2m1")


B, K, F, INCH, OUTCH, R = 2, 4, 128, 1024, 128, 128


def erf(a):
    c = np.clip(a, -6.0, 6.0)
    c2 = 2.0 * c * c
    t = c.copy()
    s = c.copy()
    n = 1.0
    while np.max(np.abs(t) - 1e-18 * np.abs(s)) > 0.0:
        n += 2.0
        t = t * c2 / n
        s = s + t
    return 2.0 / np.sqrt(np.pi) * np.exp(-c * c) * s


def gelu(t):
    return 0.5 * t * (1.0 + erf(t / np.sqrt(2.0)))


def setup_inputs():
    s = mx_kscale(INCH)
    h = bf(gelu(np.random.standard_normal((B, K, F, INCH))) * s)
    z = bf(np.random.standard_normal((B, K, F, R)) * 0.35)
    u = bf(np.random.standard_normal((B, K, OUTCH, R)) * 1.5 * np.sqrt(R))
    b = bf(np.random.standard_normal((B, 1, 1, OUTCH)) * 0.3)
    w = np.random.standard_normal((OUTCH, INCH)) * 1.5 / np.sqrt(INCH) / s
    words, scales = pack4(np.ascontiguousarray(w.T))
    b_out = bf(np.random.standard_normal(OUTCH) * 0.3)
    return {
        "h": h,
        "z": z,
        "u": u,
        "b": b,
        "W_out_words": words,
        "W_out_scales": scales,
        "b_out": b_out,
    }


def reference(h, z, u, b, W_out_words, W_out_scales, b_out):
    lora = f64(z) @ f64(u).transpose(0, 1, 3, 2) / R
    main = mxq(f64(h), 3, "e4m3") @ unpack4(W_out_words, W_out_scales)
    return gelu(main + f64(b_out) + lora + f64(b))

@@ -1,0 +1,201 @@
+import concourse.mybir as mybir
+from concourse.masks import make_identity
+
+F32 = mybir.dt.float32
+BF16 = mybir.dt.bfloat16
+I32 = mybir.dt.int32
+U32 = mybir.dt.uint32
+U8 = mybir.dt.uint8
+FP8X4 = mybir.dt.float8_e4m3fn_x4
+FP4X4 = mybir.dt.float4_e2m1fn_x4
+ADD = mybir.AluOpType.add
+MULT = mybir.AluOpType.mult
+GELU = mybir.ActivationFunctionType.Gelu
+
+P = 128
+BATCHES = 2
+MEMBERS = 4
+TILES = BATCHES * MEMBERS
+ROWS = 128
+INCH = 1024
+OUTCH = 128
+RANK = 128
+PACK = 4
+K_PASS = P * PACK
+PASSES = INCH // K_PASS
+PAIRS = PACK // 2
+WORDS_PASS = K_PASS // 2
+QUADRANTS = 4
+GROUP = 2
+GROUPS = TILES // GROUP
+PSUM_BANKS = 8
+
+FLOPS = 2 * TILES * ROWS * OUTCH * (INCH + RANK)
+
+
+def tile_loratacmlp4_pb_s_kernel(tc, h, z, u, b, W_out_words, W_out_scales, b_out, out):
+    nc = tc.nc
+    h_tiles = h.rearrange("b k f i -> (b k) f i")
+    z_rows = z.rearrange("b k f r -> f (b k) r")
+    u_rows = u.rearrange("b k o r -> o (b k) r")
+    out_rows = out.rearrange("b k f o -> f (b k) o")
+
+    with (
+        tc.tile_pool(name="keep", bufs=1) as keep,
+        tc.tile_pool(name="h_pool", bufs=TILES) as h_pool,
+        tc.tile_pool(name="work", bufs=2 * GROUP) as work,
+        tc.psum_pool(name="psum", bufs=PSUM_BANKS) as psum,
+        tc.manual_schedule(),
+    ):
+        w_scales = keep.tile([P, PASSES, OUTCH], U8, align_bytes=64)
+        nc.vector.memset(w_scales[:].bitcast(I32), 0)
+        gelu_seed = keep.tile([P, 1], F32)
+        nc.vector.memset(gelu_seed[:], 0.0)
+        bias_rows = keep.tile([P, BATCHES, OUTCH], BF16)
+        nc.vector.memset(bias_rows[:], 0.0)
+        ones = keep.tile([P, P], BF16)
+        nc.vector.memset(ones[:], 1.0)
+        ident_bf16 = keep.tile([P, P], BF16)
+        make_identity(nc, ident_bf16[:])
+        ident_f32 = keep.tile([P, P], F32)
+        make_identity(nc, ident_f32[:])
+        gelu_warm = keep.tile([P, 1], F32)
+        nc.scalar.activation(out=gelu_warm[:], in_=gelu_seed[:], func=GELU)
+
+        z_sb = keep.tile([P, TILES, RANK], BF16)
+        nc.sync.dma_start(out=z_sb[:], in_=z_rows)
+        u_sb = keep.tile([P, TILES, RANK], BF16)
+        nc.sync.dma_start(out=u_sb[:], in_=u_rows)
+
+        h_sb = []
+
+        def load_h(j):
+            h_tile = h_pool.tile([P, INCH], BF16)
+            nc.sync.dma_start(out=h_tile[:], in_=h_tiles[j])
+            h_sb.append(h_tile)
+
+        for j in range(GROUP):
+            load_h(j)
+        w_words = keep.tile([P, PASSES, 2 * OUTCH], U8, align_bytes=64)
+        nc.sync.dma_start(
+            out=w_words[:].bitcast(I32), in_=W_out_words.rearrange("g p c -> p g c").bitcast(I32)
+        )
+        for q in range(QUADRANTS):
+            nc.sync.dma_start(
+                out=w_scales[32 * q : 32 * q + 4, :, :].bitcast(I32),
+                in_=W_out_scales[:, 4 * q : 4 * q + 4, :].rearrange("g r n -> r g n").bitcast(I32),
+            )
+        for j in range(GROUP, TILES):
+            load_h(j)
+        nc.gpsimd.dma_start(out=bias_rows[0:1, :, :], in_=b.rearrange("b x y o -> (x y) b o"))
+        nc.gpsimd.dma_start(
+            out=bias_rows[1:2, :, :],
+            in_=b_out.rearrange("(x y o) -> x y o", x=1, y=1).to_broadcast([1, BATCHES, OUTCH]),
+        )
+
+        zT_sb = keep.tile([P, TILES, ROWS], BF16)
+        uT_sb = keep.tile([P, TILES, OUTCH], BF16)
+        addend = keep.tile([P, TILES, OUTCH], F32)
+        h_codes = keep.tile([P, TILES, PASSES * ROWS], U32, align_bytes=64)
+        h_scales = keep.tile([P, TILES, PASSES * ROWS], U8, align_bytes=64)
+
+        def transpose_factor(factor_sb, factorT_sb):
+            factorT_ps = psum.tile([P, TILES, P], BF16, tag="bank")
+            for j in range(TILES):
+                nc.tensor.transpose(factorT_ps[:, j, :], factor_sb[:, j, :], ident_bf16[:])
+            nc.vector.tensor_copy(out=factorT_sb[:], in_=factorT_ps[:])
+
+        def low_rank_addend():
+            bias_ps = psum.tile([P, BATCHES, OUTCH], F32, tag="bank")
+            nc.tensor.matmul(
+                out=bias_ps[:].rearrange("p b o -> p (b o)"),
+                lhsT=ones[:],
+                rhs=bias_rows[:].rearrange("p b o -> p (b o)"),
+                start=True,
+                stop=True,
+            )
+            bias_sb = keep.tile([P, BATCHES, OUTCH], F32)
+            nc.vector.tensor_copy(out=bias_sb[:], in_=bias_ps[:])
+            for batch in range(BATCHES):
+                lora_ps = psum.tile([P, MEMBERS, OUTCH], F32, tag="bank")
+                for k in range(MEMBERS):
+                    j = batch * MEMBERS + k
+                    nc.tensor.matmul(
+                        out=lora_ps[:, k, :], lhsT=zT_sb[:, j, :], rhs=uT_sb[:, j, :], start=True, stop=True
+                    )
+                nc.vector.scalar_tensor_tensor(
+                    out=addend[:, batch * MEMBERS : (batch + 1) * MEMBERS, :],
+                    in0=lora_ps[:],
+                    scalar=1.0 / RANK,
+                    in1=bias_sb[:, batch, :].unsqueeze(1).to_broadcast([P, MEMBERS, OUTCH]),
+                    op0=MULT,
+                    op1=ADD,
+                )
+
+        def transpose_h(j):
+            h_words = h_sb[j][:].bitcast(F32)
+            hT_ps = psum.tile([P, PASSES, PAIRS, ROWS], F32, tag="bank")
+            for g in range(PASSES):
+                for w in range(PAIRS):
+                    nc.tensor.transpose(
+                        hT_ps[:, g, w, :],
+                        h_words[:, g * WORDS_PASS + w : (g + 1) * WORDS_PASS : PAIRS],
+                        ident_f32[:],
+                    )
+            return hT_ps
+
+        def regroup_h(hT_ps):
+            grouped = work.tile([P, PASSES, ROWS, PACK], BF16, align_bytes=64)
+            nc.scalar.copy(out=grouped[:].bitcast(F32), in_=hT_ps[:].rearrange("p g w f -> p g f w"))
+            return grouped
+
+        def quantise_h(j, grouped):
+            nc.vector.quantize_mx(
+                out=h_codes[:, j, :].bitcast(FP8X4),
+                scales=h_scales[:, j, :],
+                in_=grouped[:].rearrange("p g f t -> p (g f t)"),
+            )
+
+        def multiply(n):
+            main_ps = psum.tile([P, GROUP, OUTCH], F32, tag="bank")
+            for i in range(GROUP):
+                j = n * GROUP + i
+                for g in range(PASSES):
+                    rows = slice(g * ROWS, (g + 1) * ROWS)
+                    nc.tensor.matmul_mx(
+                        out=main_ps[:, i, :],
+                        lhsT=h_codes[:, j, rows].bitcast(FP8X4),
+                        lhsT_scale=h_scales[:, j, rows],
+                        rhs=w_words[:, g, :].bitcast(FP4X4),
+                        rhs_scale=w_scales[:, g, :],
+                        start=(g == 0),
+                        stop=(g == PASSES - 1),
+                    )
+            return main_ps
+
+        def add_up(n, main_ps):
+            total = work.tile([P, GROUP, OUTCH], F32)
+            nc.vector.tensor_tensor(
+                out=total[:], in0=main_ps[:], in1=addend[:, n * GROUP : (n + 1) * GROUP, :], op=ADD
+            )
+            return total
+
+        def gelu_and_store(n, total):
+            result = work.tile([P, GROUP, OUTCH], F32)
+            nc.scalar.activation(out=result[:], in_=total[:], func=GELU)
+            nc.sync.dma_start(out=out_rows[:, n * GROUP : (n + 1) * GROUP, :], in_=result[:])
+
+        transpose_factor(z_sb, zT_sb)
+        transpose_factor(u_sb, uT_sb)
+        for n in range(GROUPS + 1):
+            tiles = range(n * GROUP, (n + 1) * GROUP) if n < GROUPS else []
+            banks = [transpose_h(j) for j in tiles]
+            regrouped = [regroup_h(hT_ps) for hT_ps in banks]
+            if n > 0:
+                total = add_up(n - 1, multiply(n - 1))
+            for j, grouped in zip(tiles, regrouped):
+                quantise_h(j, grouped)
+            if n == 0:
+                low_rank_addend()
+            else:
+                gelu_and_store(n - 1, total)

@@ -26,8 +26,10 @@ PASSES = INCH // K_PASS
 PAIRS = PACK // 2
 WORDS_PASS = K_PASS // 2
 QUADRANTS = 4
+FOLD = TILES * ROWS // P
 GROUP = 2
 GROUPS = TILES // GROUP
+LATE_TILES = 2
 PSUM_BANKS = 8
 
 FLOPS = 2 * TILES * ROWS * OUTCH * (INCH + RANK)
@@ -36,8 +38,8 @@ FLOPS = 2 * TILES * ROWS * OUTCH * (INCH + RANK)
 def tile_loratacmlp4_pb_s_kernel(tc, h, z, u, b, W_out_words, W_out_scales, b_out, out):
     nc = tc.nc
     h_tiles = h.rearrange("b k f i -> (b k) f i")
-    z_rows = z.rearrange("b k f r -> f (b k) r")
-    u_rows = u.rearrange("b k o r -> o (b k) r")
+    z_folded = z.rearrange("b k f r -> (b k f) r").rearrange("(p s) r -> p s r", s=FOLD)
+    u_folded = u.rearrange("b k o r -> (b k o) r").rearrange("(p s) r -> p s r", s=FOLD)
     out_rows = out.rearrange("b k f o -> f (b k) o")
 
     with (
@@ -47,6 +49,9 @@ def tile_loratacmlp4_pb_s_kernel(tc, h, z, u, b, W_out_words, W_out_scales, b_ou
         tc.psum_pool(name="psum", bufs=PSUM_BANKS) as psum,
         tc.manual_schedule(),
     ):
+        ident_f32 = keep.tile([P, P], F32)
+        nc.vector.memset(ident_f32[:], 0.0)
+        make_identity(nc, ident_f32[:], nomemset=True)
         w_scales = keep.tile([P, PASSES, OUTCH], U8, align_bytes=64)
         nc.vector.memset(w_scales[:].bitcast(I32), 0)
         gelu_seed = keep.tile([P, 1], F32)
@@ -56,16 +61,14 @@ def tile_loratacmlp4_pb_s_kernel(tc, h, z, u, b, W_out_words, W_out_scales, b_ou
         ones = keep.tile([P, P], BF16)
         nc.vector.memset(ones[:], 1.0)
         ident_bf16 = keep.tile([P, P], BF16)
-        make_identity(nc, ident_bf16[:])
-        ident_f32 = keep.tile([P, P], F32)
-        make_identity(nc, ident_f32[:])
+        nc.vector.tensor_copy(out=ident_bf16[:], in_=ident_f32[:])
         gelu_warm = keep.tile([P, 1], F32)
         nc.scalar.activation(out=gelu_warm[:], in_=gelu_seed[:], func=GELU)
 
-        z_sb = keep.tile([P, TILES, RANK], BF16)
-        nc.sync.dma_start(out=z_sb[:], in_=z_rows)
-        u_sb = keep.tile([P, TILES, RANK], BF16)
-        nc.sync.dma_start(out=u_sb[:], in_=u_rows)
+        z_sb = keep.tile([P, FOLD, RANK], BF16)
+        nc.sync.dma_start(out=z_sb[:], in_=z_folded)
+        u_sb = keep.tile([P, FOLD, RANK], BF16)
+        nc.sync.dma_start(out=u_sb[:], in_=u_folded)
 
         h_sb = []
 
@@ -74,7 +77,7 @@ def tile_loratacmlp4_pb_s_kernel(tc, h, z, u, b, W_out_words, W_out_scales, b_ou
             nc.sync.dma_start(out=h_tile[:], in_=h_tiles[j])
             h_sb.append(h_tile)
 
-        for j in range(GROUP):
+        for j in range(TILES - LATE_TILES):
             load_h(j)
         w_words = keep.tile([P, PASSES, 2 * OUTCH], U8, align_bytes=64)
         nc.sync.dma_start(
@@ -85,7 +88,7 @@ def tile_loratacmlp4_pb_s_kernel(tc, h, z, u, b, W_out_words, W_out_scales, b_ou
                 out=w_scales[32 * q : 32 * q + 4, :, :].bitcast(I32),
                 in_=W_out_scales[:, 4 * q : 4 * q + 4, :].rearrange("g r n -> r g n").bitcast(I32),
             )
-        for j in range(GROUP, TILES):
+        for j in range(TILES - LATE_TILES, TILES):
             load_h(j)
         nc.gpsimd.dma_start(out=bias_rows[0:1, :, :], in_=b.rearrange("b x y o -> (x y) b o"))
         nc.gpsimd.dma_start(
@@ -93,17 +96,20 @@ def tile_loratacmlp4_pb_s_kernel(tc, h, z, u, b, W_out_words, W_out_scales, b_ou
             in_=b_out.rearrange("(x y o) -> x y o", x=1, y=1).to_broadcast([1, BATCHES, OUTCH]),
         )
 
-        zT_sb = keep.tile([P, TILES, ROWS], BF16)
-        uT_sb = keep.tile([P, TILES, OUTCH], BF16)
+        zT_sb = keep.tile([P, TILES * ROWS], BF16)
+        uT_sb = keep.tile([P, TILES * OUTCH], BF16)
         addend = keep.tile([P, TILES, OUTCH], F32)
         h_codes = keep.tile([P, TILES, PASSES * ROWS], U32, align_bytes=64)
         h_scales = keep.tile([P, TILES, PASSES * ROWS], U8, align_bytes=64)
 
         def transpose_factor(factor_sb, factorT_sb):
-            factorT_ps = psum.tile([P, TILES, P], BF16, tag="bank")
-            for j in range(TILES):
-                nc.tensor.transpose(factorT_ps[:, j, :], factor_sb[:, j, :], ident_bf16[:])
-            nc.vector.tensor_copy(out=factorT_sb[:], in_=factorT_ps[:])
+            factorT_ps = psum.tile([P, FOLD, P], BF16, tag="bank")
+            for s in range(FOLD):
+                nc.tensor.transpose(factorT_ps[:, s, :], factor_sb[:, s, :], ident_bf16[:])
+            nc.vector.tensor_copy(
+                out=factorT_sb[:].rearrange("r (p s) -> r p s", s=FOLD),
+                in_=factorT_ps[:].rearrange("r s p -> r p s"),
+            )
 
         def low_rank_addend():
             bias_ps = psum.tile([P, BATCHES, OUTCH], F32, tag="bank")
@@ -121,7 +127,11 @@ def tile_loratacmlp4_pb_s_kernel(tc, h, z, u, b, W_out_words, W_out_scales, b_ou
                 for k in range(MEMBERS):
                     j = batch * MEMBERS + k
                     nc.tensor.matmul(
-                        out=lora_ps[:, k, :], lhsT=zT_sb[:, j, :], rhs=uT_sb[:, j, :], start=True, stop=True
+                        out=lora_ps[:, k, :],
+                        lhsT=zT_sb[:, j * ROWS : (j + 1) * ROWS],
+                        rhs=uT_sb[:, j * OUTCH : (j + 1) * OUTCH],
+                        start=True,
+                        stop=True,
                     )
                 nc.vector.scalar_tensor_tensor(
                     out=addend[:, batch * MEMBERS : (batch + 1) * MEMBERS, :],
@@ -185,17 +195,15 @@ def tile_loratacmlp4_pb_s_kernel(tc, h, z, u, b, W_out_words, W_out_scales, b_ou
             nc.scalar.activation(out=result[:], in_=total[:], func=GELU)
             nc.sync.dma_start(out=out_rows[:, n * GROUP : (n + 1) * GROUP, :], in_=result[:])
 
+        def prepare_h(j):
+            quantise_h(j, regroup_h(transpose_h(j)))
+
         transpose_factor(z_sb, zT_sb)
         transpose_factor(u_sb, uT_sb)
-        for n in range(GROUPS + 1):
-            tiles = range(n * GROUP, (n + 1) * GROUP) if n < GROUPS else []
-            banks = [transpose_h(j) for j in tiles]
-            regrouped = [regroup_h(hT_ps) for hT_ps in banks]
-            if n > 0:
-                total = add_up(n - 1, multiply(n - 1))
-            for j, grouped in zip(tiles, regrouped):
-                quantise_h(j, grouped)
-            if n == 0:
-                low_rank_addend()
-            else:
-                gelu_and_store(n - 1, total)
+        for j in range(TILES // 2):
+            prepare_h(j)
+        low_rank_addend()
+        for j in range(TILES // 2, TILES):
+            prepare_h(j)
+        for n in range(GROUPS):
+            gelu_and_store(n, add_up(n, multiply(n)))

@@ -203,7 +203,11 @@ def tile_loratacmlp4_pb_s_kernel(tc, h, z, u, b, W_out_words, W_out_scales, b_ou
         for j in range(TILES // 2):
             prepare_h(j)
         low_rank_addend()
-        for j in range(TILES // 2, TILES):
+        for j in range(TILES // 2, TILES - 1):
             prepare_h(j)
-        for n in range(GROUPS):
+        grouped_last = regroup_h(transpose_h(TILES - 1))
+        total_first = add_up(0, multiply(0))
+        quantise_h(TILES - 1, grouped_last)
+        gelu_and_store(0, total_first)
+        for n in range(1, GROUPS):
             gelu_and_store(n, add_up(n, multiply(n)))

@@ -144,11 +144,11 @@ def tile_loratacmlp4_pb_s_kernel(tc, h, z, u, b, W_out_words, W_out_scales, b_ou
 
         def transpose_h(j):
             h_words = h_sb[j][:].bitcast(F32)
-            hT_ps = psum.tile([P, PASSES, PAIRS, ROWS], F32, tag="bank")
+            hT_ps = psum.tile([P, PAIRS, PASSES, ROWS], F32, tag="bank")
             for g in range(PASSES):
                 for w in range(PAIRS):
                     nc.tensor.transpose(
-                        hT_ps[:, g, w, :],
+                        hT_ps[:, w, g, :],
                         h_words[:, g * WORDS_PASS + w : (g + 1) * WORDS_PASS : PAIRS],
                         ident_f32[:],
                     )
@@ -156,7 +156,10 @@ def tile_loratacmlp4_pb_s_kernel(tc, h, z, u, b, W_out_words, W_out_scales, b_ou
 
         def regroup_h(hT_ps):
             grouped = work.tile([P, PASSES, ROWS, PACK], BF16, align_bytes=64)
-            nc.scalar.copy(out=grouped[:].bitcast(F32), in_=hT_ps[:].rearrange("p g w f -> p g f w"))
+            nc.scalar.copy(
+                out=grouped[:].bitcast(F32).rearrange("p g (c i) w -> p (g c) w i", i=2),
+                in_=hT_ps[:].rearrange("p w g (c i) -> p (g c) w i", i=2),
+            )
             return grouped
 
         def quantise_h(j, grouped):

@@ -31,6 +31,8 @@ GROUP = 2
 GROUPS = TILES // GROUP
 LATE_TILES = 2
 PSUM_BANKS = 8
+Z_PIECES = (2, 2, 4)
+U_PIECES = (4, 4)
 
 FLOPS = 2 * TILES * ROWS * OUTCH * (INCH + RANK)
 
@@ -45,6 +47,7 @@ def tile_loratacmlp4_pb_s_kernel(tc, h, z, u, b, W_out_words, W_out_scales, b_ou
     with (
         tc.tile_pool(name="keep", bufs=1) as keep,
         tc.tile_pool(name="h_pool", bufs=TILES) as h_pool,
+        tc.tile_pool(name="factor_pool", bufs=len(Z_PIECES) + len(U_PIECES)) as factor_pool,
         tc.tile_pool(name="work", bufs=2 * GROUP) as work,
         tc.psum_pool(name="psum", bufs=PSUM_BANKS) as psum,
         tc.manual_schedule(),
@@ -65,10 +68,16 @@ def tile_loratacmlp4_pb_s_kernel(tc, h, z, u, b, W_out_words, W_out_scales, b_ou
         gelu_warm = keep.tile([P, 1], F32)
         nc.scalar.activation(out=gelu_warm[:], in_=gelu_seed[:], func=GELU)
 
-        z_sb = keep.tile([P, FOLD, RANK], BF16)
-        nc.sync.dma_start(out=z_sb[:], in_=z_folded)
-        u_sb = keep.tile([P, FOLD, RANK], BF16)
-        nc.sync.dma_start(out=u_sb[:], in_=u_folded)
+        def load_factor(folded, piece_slots):
+            slots = []
+            for count in piece_slots:
+                piece = factor_pool.tile([P, count, RANK], BF16)
+                nc.sync.dma_start(out=piece[:], in_=folded[:, len(slots) : len(slots) + count, :])
+                slots.extend([piece[:, i, :] for i in range(count)])
+            return slots
+
+        z_slots = load_factor(z_folded, Z_PIECES)
+        u_slots = load_factor(u_folded, U_PIECES)
 
         h_sb = []
 
@@ -102,10 +111,10 @@ def tile_loratacmlp4_pb_s_kernel(tc, h, z, u, b, W_out_words, W_out_scales, b_ou
         h_codes = keep.tile([P, TILES, PASSES * ROWS], U32, align_bytes=64)
         h_scales = keep.tile([P, TILES, PASSES * ROWS], U8, align_bytes=64)
 
-        def transpose_factor(factor_sb, factorT_sb):
+        def transpose_factor(factor_slots, factorT_sb):
             factorT_ps = psum.tile([P, FOLD, P], BF16, tag="bank")
             for s in range(FOLD):
-                nc.tensor.transpose(factorT_ps[:, s, :], factor_sb[:, s, :], ident_bf16[:])
+                nc.tensor.transpose(factorT_ps[:, s, :], factor_slots[s], ident_bf16[:])
             nc.vector.tensor_copy(
                 out=factorT_sb[:].rearrange("r (p s) -> r p s", s=FOLD),
                 in_=factorT_ps[:].rearrange("r s p -> r p s"),
@@ -201,8 +210,8 @@ def tile_loratacmlp4_pb_s_kernel(tc, h, z, u, b, W_out_words, W_out_scales, b_ou
         def prepare_h(j):
             quantise_h(j, regroup_h(transpose_h(j)))
 
-        transpose_factor(z_sb, zT_sb)
-        transpose_factor(u_sb, uT_sb)
+        transpose_factor(z_slots, zT_sb)
+        transpose_factor(u_slots, uT_sb)
         for j in range(TILES // 2):
             prepare_h(j)
         low_rank_addend()

@@ -50,7 +50,6 @@ def tile_loratacmlp4_pb_s_kernel(tc, h, z, u, b, W_out_words, W_out_scales, b_ou
         tc.tile_pool(name="factor_pool", bufs=len(Z_PIECES) + len(U_PIECES)) as factor_pool,
         tc.tile_pool(name="work", bufs=2 * GROUP) as work,
         tc.psum_pool(name="psum", bufs=PSUM_BANKS) as psum,
-        tc.manual_schedule(),
     ):
         ident_f32 = keep.tile([P, P], F32)
         nc.vector.memset(ident_f32[:], 0.0)

@@ -31,6 +31,7 @@ GROUP = 2
 GROUPS = TILES // GROUP
 LATE_TILES = 2
 PSUM_BANKS = 8
+WARM_PASSES = 7
 Z_PIECES = (2, 2, 4)
 U_PIECES = (4, 4)
 
@@ -51,11 +52,28 @@ def tile_loratacmlp4_pb_s_kernel(tc, h, z, u, b, W_out_words, W_out_scales, b_ou
         tc.tile_pool(name="work", bufs=2 * GROUP) as work,
         tc.psum_pool(name="psum", bufs=PSUM_BANKS) as psum,
     ):
-        ident_f32 = keep.tile([P, P], F32)
-        nc.vector.memset(ident_f32[:], 0.0)
-        make_identity(nc, ident_f32[:], nomemset=True)
+        w_words = keep.tile([P, PASSES, 2 * OUTCH], U8, align_bytes=64)
         w_scales = keep.tile([P, PASSES, OUTCH], U8, align_bytes=64)
+        h_codes = keep.tile([P, TILES, PASSES * ROWS], U32, align_bytes=64)
+        h_scales = keep.tile([P, TILES, PASSES * ROWS], U8, align_bytes=64)
+        warm_rows = slice(0, ROWS)
+        nc.vector.memset(h_codes[:, TILES - 1, warm_rows], 0)
+        nc.vector.memset(w_words[:].bitcast(I32), 0)
+        nc.vector.memset(h_scales[:, TILES - 1, warm_rows].bitcast(I32), 0)
         nc.vector.memset(w_scales[:].bitcast(I32), 0)
+        warm_ps = psum.tile([P, PASSES * OUTCH], F32, tag="bank")
+        for i in range(WARM_PASSES):
+            nc.tensor.matmul_mx(
+                out=warm_ps[:],
+                lhsT=h_codes[:, TILES - 1, warm_rows].bitcast(FP8X4),
+                lhsT_scale=h_scales[:, TILES - 1, warm_rows],
+                rhs=w_words[:].rearrange("p g c -> p (g c)").bitcast(FP4X4),
+                rhs_scale=w_scales[:].rearrange("p g n -> p (g n)"),
+                start=True,
+                stop=True,
+            )
+        ident_f32 = keep.tile([P, P], F32)
+        make_identity(nc, ident_f32[:])
         gelu_seed = keep.tile([P, 1], F32)
         nc.vector.memset(gelu_seed[:], 0.0)
         bias_rows = keep.tile([P, BATCHES, OUTCH], BF16)
@@ -87,7 +105,6 @@ def tile_loratacmlp4_pb_s_kernel(tc, h, z, u, b, W_out_words, W_out_scales, b_ou
 
         for j in range(TILES - LATE_TILES):
             load_h(j)
-        w_words = keep.tile([P, PASSES, 2 * OUTCH], U8, align_bytes=64)
         nc.sync.dma_start(
             out=w_words[:].bitcast(I32), in_=W_out_words.rearrange("g p c -> p g c").bitcast(I32)
         )
@@ -107,8 +124,6 @@ def tile_loratacmlp4_pb_s_kernel(tc, h, z, u, b, W_out_words, W_out_scales, b_ou
         zT_sb = keep.tile([P, TILES * ROWS], BF16)
         uT_sb = keep.tile([P, TILES * OUTCH], BF16)
         addend = keep.tile([P, TILES, OUTCH], F32)
-        h_codes = keep.tile([P, TILES, PASSES * ROWS], U32, align_bytes=64)
-        h_scales = keep.tile([P, TILES, PASSES * ROWS], U8, align_bytes=64)
 
         def transpose_factor(factor_slots, factorT_sb):
             factorT_ps = psum.tile([P, FOLD, P], BF16, tag="bank")

@@ -51,6 +51,7 @@ def tile_loratacmlp4_pb_s_kernel(tc, h, z, u, b, W_out_words, W_out_scales, b_ou
         tc.tile_pool(name="factor_pool", bufs=len(Z_PIECES) + len(U_PIECES)) as factor_pool,
         tc.tile_pool(name="work", bufs=2 * GROUP) as work,
         tc.psum_pool(name="psum", bufs=PSUM_BANKS) as psum,
+        tc.manual_schedule(),
     ):
         w_words = keep.tile([P, PASSES, 2 * OUTCH], U8, align_bytes=64)
         w_scales = keep.tile([P, PASSES, OUTCH], U8, align_bytes=64)
@@ -72,12 +73,17 @@ def tile_loratacmlp4_pb_s_kernel(tc, h, z, u, b, W_out_words, W_out_scales, b_ou
                 start=True,
                 stop=True,
             )
-        ident_f32 = keep.tile([P, P], F32)
-        make_identity(nc, ident_f32[:])
         gelu_seed = keep.tile([P, 1], F32)
         nc.vector.memset(gelu_seed[:], 0.0)
+        ident_f32 = keep.tile([P, P], F32)
         bias_rows = keep.tile([P, BATCHES, OUTCH], BF16)
-        nc.vector.memset(bias_rows[:], 0.0)
+        nc.gpsimd.memset(bias_rows[:], 0.0)
+        nc.scalar.dma_start(out=bias_rows[0:1, :, :], in_=b.rearrange("b x y o -> (x y) b o"))
+        nc.scalar.dma_start(
+            out=bias_rows[1:2, :, :],
+            in_=b_out.rearrange("(x y o) -> x y o", x=1, y=1).to_broadcast([1, BATCHES, OUTCH]),
+        )
+        make_identity(nc, ident_f32[:])
         ones = keep.tile([P, P], BF16)
         nc.vector.memset(ones[:], 1.0)
         ident_bf16 = keep.tile([P, P], BF16)
@@ -115,11 +121,6 @@ def tile_loratacmlp4_pb_s_kernel(tc, h, z, u, b, W_out_words, W_out_scales, b_ou
             )
         for j in range(TILES - LATE_TILES, TILES):
             load_h(j)
-        nc.gpsimd.dma_start(out=bias_rows[0:1, :, :], in_=b.rearrange("b x y o -> (x y) b o"))
-        nc.gpsimd.dma_start(
-            out=bias_rows[1:2, :, :],
-            in_=b_out.rearrange("(x y o) -> x y o", x=1, y=1).to_broadcast([1, BATCHES, OUTCH]),
-        )
 
         zT_sb = keep.tile([P, TILES * ROWS], BF16)
         uT_sb = keep.tile([P, TILES * OUTCH], BF16)
@@ -134,7 +135,9 @@ def tile_loratacmlp4_pb_s_kernel(tc, h, z, u, b, W_out_words, W_out_scales, b_ou
                 in_=factorT_ps[:].rearrange("r s p -> r p s"),
             )
 
-        def low_rank_addend():
+        bias_sb = keep.tile([P, BATCHES, OUTCH], F32)
+
+        def spread_bias():
             bias_ps = psum.tile([P, BATCHES, OUTCH], F32, tag="bank")
             nc.tensor.matmul(
                 out=bias_ps[:].rearrange("p b o -> p (b o)"),
@@ -143,27 +146,27 @@ def tile_loratacmlp4_pb_s_kernel(tc, h, z, u, b, W_out_words, W_out_scales, b_ou
                 start=True,
                 stop=True,
             )
-            bias_sb = keep.tile([P, BATCHES, OUTCH], F32)
             nc.vector.tensor_copy(out=bias_sb[:], in_=bias_ps[:])
-            for batch in range(BATCHES):
-                lora_ps = psum.tile([P, MEMBERS, OUTCH], F32, tag="bank")
-                for k in range(MEMBERS):
-                    j = batch * MEMBERS + k
-                    nc.tensor.matmul(
-                        out=lora_ps[:, k, :],
-                        lhsT=zT_sb[:, j * ROWS : (j + 1) * ROWS],
-                        rhs=uT_sb[:, j * OUTCH : (j + 1) * OUTCH],
-                        start=True,
-                        stop=True,
-                    )
-                nc.vector.scalar_tensor_tensor(
-                    out=addend[:, batch * MEMBERS : (batch + 1) * MEMBERS, :],
-                    in0=lora_ps[:],
-                    scalar=1.0 / RANK,
-                    in1=bias_sb[:, batch, :].unsqueeze(1).to_broadcast([P, MEMBERS, OUTCH]),
-                    op0=MULT,
-                    op1=ADD,
+
+        def low_rank_addend(batch):
+            lora_ps = psum.tile([P, MEMBERS, OUTCH], F32, tag="bank")
+            for k in range(MEMBERS):
+                j = batch * MEMBERS + k
+                nc.tensor.matmul(
+                    out=lora_ps[:, k, :],
+                    lhsT=zT_sb[:, j * ROWS : (j + 1) * ROWS],
+                    rhs=uT_sb[:, j * OUTCH : (j + 1) * OUTCH],
+                    start=True,
+                    stop=True,
                 )
+            nc.vector.scalar_tensor_tensor(
+                out=addend[:, batch * MEMBERS : (batch + 1) * MEMBERS, :],
+                in0=lora_ps[:],
+                scalar=1.0 / RANK,
+                in1=bias_sb[:, batch, :].unsqueeze(1).to_broadcast([P, MEMBERS, OUTCH]),
+                op0=MULT,
+                op1=ADD,
+            )
 
         def transpose_h(j):
             h_words = h_sb[j][:].bitcast(F32)
@@ -226,11 +229,14 @@ def tile_loratacmlp4_pb_s_kernel(tc, h, z, u, b, W_out_words, W_out_scales, b_ou
 
         transpose_factor(z_slots, zT_sb)
         transpose_factor(u_slots, uT_sb)
-        for j in range(TILES // 2):
+        for j in range(3):
             prepare_h(j)
-        low_rank_addend()
-        for j in range(TILES // 2, TILES - 1):
+        spread_bias()
+        low_rank_addend(0)
+        for j in range(3, 6):
             prepare_h(j)
+        low_rank_addend(1)
+        prepare_h(6)
         grouped_last = regroup_h(transpose_h(TILES - 1))
         total_first = add_up(0, multiply(0))
         quantise_h(TILES - 1, grouped_last)

@@ -32,8 +32,7 @@ GROUPS = TILES // GROUP
 LATE_TILES = 2
 PSUM_BANKS = 8
 WARM_PASSES = 7
-Z_PIECES = (2, 2, 4)
-U_PIECES = (4, 4)
+EARLY_TILES = 2
 
 FLOPS = 2 * TILES * ROWS * OUTCH * (INCH + RANK)
 
@@ -48,7 +47,7 @@ def tile_loratacmlp4_pb_s_kernel(tc, h, z, u, b, W_out_words, W_out_scales, b_ou
     with (
         tc.tile_pool(name="keep", bufs=1) as keep,
         tc.tile_pool(name="h_pool", bufs=TILES) as h_pool,
-        tc.tile_pool(name="factor_pool", bufs=len(Z_PIECES) + len(U_PIECES)) as factor_pool,
+        tc.tile_pool(name="factor_pool", bufs=2) as factor_pool,
         tc.tile_pool(name="work", bufs=2 * GROUP) as work,
         tc.psum_pool(name="psum", bufs=PSUM_BANKS) as psum,
         tc.manual_schedule(),
@@ -91,25 +90,27 @@ def tile_loratacmlp4_pb_s_kernel(tc, h, z, u, b, W_out_words, W_out_scales, b_ou
         gelu_warm = keep.tile([P, 1], F32)
         nc.scalar.activation(out=gelu_warm[:], in_=gelu_seed[:], func=GELU)
 
-        def load_factor(folded, piece_slots):
-            slots = []
-            for count in piece_slots:
-                piece = factor_pool.tile([P, count, RANK], BF16)
-                nc.sync.dma_start(out=piece[:], in_=folded[:, len(slots) : len(slots) + count, :])
-                slots.extend([piece[:, i, :] for i in range(count)])
-            return slots
-
-        z_slots = load_factor(z_folded, Z_PIECES)
-        u_slots = load_factor(u_folded, U_PIECES)
+        def load_factor(folded):
+            factor_tile = factor_pool.tile([P, FOLD, RANK], BF16)
+            nc.sync.dma_start(out=factor_tile[:], in_=folded)
+            return [factor_tile[:, s, :] for s in range(FOLD)]
 
         h_sb = []
 
-        def load_h(j):
+        def load_h(j, pieces=1):
             h_tile = h_pool.tile([P, INCH], BF16)
-            nc.sync.dma_start(out=h_tile[:], in_=h_tiles[j])
+            width = INCH // pieces
+            for i in range(pieces):
+                cols = slice(i * width, (i + 1) * width)
+                nc.sync.dma_start(out=h_tile[:, cols], in_=h_tiles[j][:, cols])
             h_sb.append(h_tile)
 
-        for j in range(TILES - LATE_TILES):
+        load_h(0, pieces=PASSES)
+        for j in range(1, EARLY_TILES):
+            load_h(j)
+        z_slots = load_factor(z_folded)
+        u_slots = load_factor(u_folded)
+        for j in range(EARLY_TILES, TILES - LATE_TILES):
             load_h(j)
         nc.sync.dma_start(
             out=w_words[:].bitcast(I32), in_=W_out_words.rearrange("g p c -> p g c").bitcast(I32)
@@ -126,14 +127,17 @@ def tile_loratacmlp4_pb_s_kernel(tc, h, z, u, b, W_out_words, W_out_scales, b_ou
         uT_sb = keep.tile([P, TILES * OUTCH], BF16)
         addend = keep.tile([P, TILES, OUTCH], F32)
 
-        def transpose_factor(factor_slots, factorT_sb):
+        def transpose_factor(factor_slots, factorT_sb, copy):
             factorT_ps = psum.tile([P, FOLD, P], BF16, tag="bank")
             for s in range(FOLD):
                 nc.tensor.transpose(factorT_ps[:, s, :], factor_slots[s], ident_bf16[:])
-            nc.vector.tensor_copy(
-                out=factorT_sb[:].rearrange("r (p s) -> r p s", s=FOLD),
-                in_=factorT_ps[:].rearrange("r s p -> r p s"),
-            )
+            half = P // BATCHES
+            for batch in range(BATCHES):
+                cols = slice(batch * half, (batch + 1) * half)
+                copy(
+                    out=factorT_sb[:].rearrange("r (p s) -> r p s", s=FOLD)[:, cols, :],
+                    in_=factorT_ps[:].rearrange("r s p -> r p s")[:, cols, :],
+                )
 
         bias_sb = keep.tile([P, BATCHES, OUTCH], F32)
 
@@ -227,14 +231,16 @@ def tile_loratacmlp4_pb_s_kernel(tc, h, z, u, b, W_out_words, W_out_scales, b_ou
         def prepare_h(j):
             quantise_h(j, regroup_h(transpose_h(j)))
 
-        transpose_factor(z_slots, zT_sb)
-        transpose_factor(u_slots, uT_sb)
-        for j in range(3):
-            prepare_h(j)
+        prepare_h(0)
+        prepare_h(1)
+        transpose_factor(z_slots, zT_sb, nc.scalar.copy)
+        transpose_factor(u_slots, uT_sb, nc.vector.tensor_copy)
+        prepare_h(2)
+        prepare_h(3)
         spread_bias()
         low_rank_addend(0)
-        for j in range(3, 6):
-            prepare_h(j)
+        prepare_h(4)
+        prepare_h(5)
         low_rank_addend(1)
         prepare_h(6)
         grouped_last = regroup_h(transpose_h(TILES - 1))

@@ -27,11 +27,11 @@ PAIRS = PACK // 2
 WORDS_PASS = K_PASS // 2
 QUADRANTS = 4
 FOLD = TILES * ROWS // P
-GROUP = 2
-GROUPS = TILES // GROUP
-LATE_TILES = 2
 PSUM_BANKS = 8
-WARM_PASSES = 7
+ENDS = 5
+WARM_PASSES = 8
+WARM_AGAIN_PASSES = 2
+W_BEHIND_TILES = 6
 EARLY_TILES = 2
 
 FLOPS = 2 * TILES * ROWS * OUTCH * (INCH + RANK)
@@ -48,7 +48,8 @@ def tile_loratacmlp4_pb_s_kernel(tc, h, z, u, b, W_out_words, W_out_scales, b_ou
         tc.tile_pool(name="keep", bufs=1) as keep,
         tc.tile_pool(name="h_pool", bufs=TILES) as h_pool,
         tc.tile_pool(name="factor_pool", bufs=2) as factor_pool,
-        tc.tile_pool(name="work", bufs=2 * GROUP) as work,
+        tc.tile_pool(name="work", bufs=4) as work,
+        tc.tile_pool(name="ends", bufs=ENDS) as ends,
         tc.psum_pool(name="psum", bufs=PSUM_BANKS) as psum,
         tc.manual_schedule(),
     ):
@@ -59,19 +60,23 @@ def tile_loratacmlp4_pb_s_kernel(tc, h, z, u, b, W_out_words, W_out_scales, b_ou
         warm_rows = slice(0, ROWS)
         nc.vector.memset(h_codes[:, TILES - 1, warm_rows], 0)
         nc.vector.memset(w_words[:].bitcast(I32), 0)
-        nc.vector.memset(h_scales[:, TILES - 1, warm_rows].bitcast(I32), 0)
-        nc.vector.memset(w_scales[:].bitcast(I32), 0)
-        warm_ps = psum.tile([P, PASSES * OUTCH], F32, tag="bank")
-        for i in range(WARM_PASSES):
-            nc.tensor.matmul_mx(
-                out=warm_ps[:],
-                lhsT=h_codes[:, TILES - 1, warm_rows].bitcast(FP8X4),
-                lhsT_scale=h_scales[:, TILES - 1, warm_rows],
-                rhs=w_words[:].rearrange("p g c -> p (g c)").bitcast(FP4X4),
-                rhs_scale=w_scales[:].rearrange("p g n -> p (g n)"),
-                start=True,
-                stop=True,
-            )
+        nc.gpsimd.memset(h_scales[:, TILES - 1, warm_rows].bitcast(I32), 0)
+        nc.gpsimd.memset(w_scales[:].bitcast(I32), 0)
+
+        def keep_warm(count):
+            warm_ps = psum.tile([P, PASSES * OUTCH], F32, tag="bank")
+            for i in range(count):
+                nc.tensor.matmul_mx(
+                    out=warm_ps[:],
+                    lhsT=h_codes[:, TILES - 1, warm_rows].bitcast(FP8X4),
+                    lhsT_scale=h_scales[:, TILES - 1, warm_rows],
+                    rhs=w_words[:].rearrange("p g c -> p (g c)").bitcast(FP4X4),
+                    rhs_scale=w_scales[:].rearrange("p g n -> p (g n)"),
+                    start=True,
+                    stop=True,
+                )
+
+        keep_warm(WARM_PASSES)
         gelu_seed = keep.tile([P, 1], F32)
         nc.vector.memset(gelu_seed[:], 0.0)
         ident_f32 = keep.tile([P, P], F32)
@@ -110,19 +115,8 @@ def tile_loratacmlp4_pb_s_kernel(tc, h, z, u, b, W_out_words, W_out_scales, b_ou
             load_h(j)
         z_slots = load_factor(z_folded)
         u_slots = load_factor(u_folded)
-        for j in range(EARLY_TILES, TILES - LATE_TILES):
+        for j in range(EARLY_TILES, W_BEHIND_TILES):
             load_h(j)
-        nc.sync.dma_start(
-            out=w_words[:].bitcast(I32), in_=W_out_words.rearrange("g p c -> p g c").bitcast(I32)
-        )
-        for q in range(QUADRANTS):
-            nc.sync.dma_start(
-                out=w_scales[32 * q : 32 * q + 4, :, :].bitcast(I32),
-                in_=W_out_scales[:, 4 * q : 4 * q + 4, :].rearrange("g r n -> r g n").bitcast(I32),
-            )
-        for j in range(TILES - LATE_TILES, TILES):
-            load_h(j)
-
         zT_sb = keep.tile([P, TILES * ROWS], BF16)
         uT_sb = keep.tile([P, TILES * OUTCH], BF16)
         addend = keep.tile([P, TILES, OUTCH], F32)
@@ -184,25 +178,30 @@ def tile_loratacmlp4_pb_s_kernel(tc, h, z, u, b, W_out_words, W_out_scales, b_ou
                     )
             return hT_ps
 
-        def regroup_h(hT_ps):
+        def regroup_h(hT_ps, pieces=1):
             grouped = work.tile([P, PASSES, ROWS, PACK], BF16, align_bytes=64)
-            nc.scalar.copy(
-                out=grouped[:].bitcast(F32).rearrange("p g (c i) w -> p (g c) w i", i=2),
-                in_=hT_ps[:].rearrange("p w g (c i) -> p (g c) w i", i=2),
-            )
+            for i in range(pieces):
+                gs = slice(i * PASSES // pieces, (i + 1) * PASSES // pieces)
+                nc.scalar.copy(
+                    out=grouped[:, gs].bitcast(F32).rearrange("p g (c i) w -> p (g c) w i", i=2),
+                    in_=hT_ps[:, :, gs].rearrange("p w g (c i) -> p (g c) w i", i=2),
+                )
             return grouped
 
-        def quantise_h(j, grouped):
-            nc.vector.quantize_mx(
-                out=h_codes[:, j, :].bitcast(FP8X4),
-                scales=h_scales[:, j, :],
-                in_=grouped[:].rearrange("p g f t -> p (g f t)"),
-            )
+        def quantise_h(j, grouped, pieces=1):
+            width = PASSES * ROWS // pieces
+            words = grouped[:].rearrange("p g f t -> p (g f t)")
+            for i in range(pieces):
+                cols = slice(i * width, (i + 1) * width)
+                nc.vector.quantize_mx(
+                    out=h_codes[:, j, cols].bitcast(FP8X4),
+                    scales=h_scales[:, j, cols],
+                    in_=words[:, PACK * i * width : PACK * (i + 1) * width],
+                )
 
-        def multiply(n):
-            main_ps = psum.tile([P, GROUP, OUTCH], F32, tag="bank")
-            for i in range(GROUP):
-                j = n * GROUP + i
+        def multiply(tiles):
+            main_ps = psum.tile([P, len(tiles), OUTCH], F32, tag="bank")
+            for i, j in enumerate(tiles):
                 for g in range(PASSES):
                     rows = slice(g * ROWS, (g + 1) * ROWS)
                     nc.tensor.matmul_mx(
@@ -216,23 +215,34 @@ def tile_loratacmlp4_pb_s_kernel(tc, h, z, u, b, W_out_words, W_out_scales, b_ou
                     )
             return main_ps
 
-        def add_up(n, main_ps):
-            total = work.tile([P, GROUP, OUTCH], F32)
+        def add_up(tiles, main_ps):
+            total = ends.tile([P, len(tiles), OUTCH], F32)
             nc.vector.tensor_tensor(
-                out=total[:], in0=main_ps[:], in1=addend[:, n * GROUP : (n + 1) * GROUP, :], op=ADD
+                out=total[:], in0=main_ps[:], in1=addend[:, tiles[0] : tiles[-1] + 1, :], op=ADD
             )
             return total
 
-        def gelu_and_store(n, total):
-            result = work.tile([P, GROUP, OUTCH], F32)
+        def gelu_and_store(tiles, total):
+            result = ends.tile([P, len(tiles), OUTCH], F32)
             nc.scalar.activation(out=result[:], in_=total[:], func=GELU)
-            nc.sync.dma_start(out=out_rows[:, n * GROUP : (n + 1) * GROUP, :], in_=result[:])
+            nc.sync.dma_start(out=out_rows[:, tiles[0] : tiles[-1] + 1, :], in_=result[:])
 
         def prepare_h(j):
             quantise_h(j, regroup_h(transpose_h(j)))
 
         prepare_h(0)
         prepare_h(1)
+        keep_warm(WARM_AGAIN_PASSES)
+        nc.sync.dma_start(
+            out=w_words[:].bitcast(I32), in_=W_out_words.rearrange("g p c -> p g c").bitcast(I32)
+        )
+        for q in range(QUADRANTS):
+            nc.sync.dma_start(
+                out=w_scales[32 * q : 32 * q + 4, :, :].bitcast(I32),
+                in_=W_out_scales[:, 4 * q : 4 * q + 4, :].rearrange("g r n -> r g n").bitcast(I32),
+            )
+        for j in range(W_BEHIND_TILES, TILES):
+            load_h(j)
         transpose_factor(z_slots, zT_sb, nc.scalar.copy)
         transpose_factor(u_slots, uT_sb, nc.vector.tensor_copy)
         prepare_h(2)
@@ -243,9 +253,12 @@ def tile_loratacmlp4_pb_s_kernel(tc, h, z, u, b, W_out_words, W_out_scales, b_ou
         prepare_h(5)
         low_rank_addend(1)
         prepare_h(6)
-        grouped_last = regroup_h(transpose_h(TILES - 1))
-        total_first = add_up(0, multiply(0))
-        quantise_h(TILES - 1, grouped_last)
-        gelu_and_store(0, total_first)
-        for n in range(1, GROUPS):
-            gelu_and_store(n, add_up(n, multiply(n)))
+        grouped_last = regroup_h(transpose_h(7), pieces=PASSES)
+        total_01 = add_up((0, 1), multiply((0, 1)))
+        gelu_and_store((0, 1), total_01)
+        main_23 = multiply((2, 3))
+        quantise_h(7, grouped_last, pieces=PASSES)
+        gelu_and_store((2, 3), add_up((2, 3), main_23))
+        gelu_and_store((4, 5), add_up((4, 5), multiply((4, 5))))
+        gelu_and_store((6,), add_up((6,), multiply((6,))))
+        gelu_and_store((7,), add_up((7,), multiply((7,))))

@@ -29,10 +29,7 @@ QUADRANTS = 4
 FOLD = TILES * ROWS // P
 PSUM_BANKS = 8
 ENDS = 5
-WARM_PASSES = 8
-WARM_AGAIN_PASSES = 2
-W_BEHIND_TILES = 6
-EARLY_TILES = 2
+WARM_PASSES = 14
 
 FLOPS = 2 * TILES * ROWS * OUTCH * (INCH + RANK)
 
@@ -59,34 +56,26 @@ def tile_loratacmlp4_pb_s_kernel(tc, h, z, u, b, W_out_words, W_out_scales, b_ou
         h_scales = keep.tile([P, TILES, PASSES * ROWS], U8, align_bytes=64)
         warm_rows = slice(0, ROWS)
         nc.vector.memset(h_codes[:, TILES - 1, warm_rows], 0)
-        nc.vector.memset(w_words[:].bitcast(I32), 0)
         nc.gpsimd.memset(h_scales[:, TILES - 1, warm_rows].bitcast(I32), 0)
-        nc.gpsimd.memset(w_scales[:].bitcast(I32), 0)
-
-        def keep_warm(count):
-            warm_ps = psum.tile([P, PASSES * OUTCH], F32, tag="bank")
-            for i in range(count):
-                nc.tensor.matmul_mx(
-                    out=warm_ps[:],
-                    lhsT=h_codes[:, TILES - 1, warm_rows].bitcast(FP8X4),
-                    lhsT_scale=h_scales[:, TILES - 1, warm_rows],
-                    rhs=w_words[:].rearrange("p g c -> p (g c)").bitcast(FP4X4),
-                    rhs_scale=w_scales[:].rearrange("p g n -> p (g n)"),
-                    start=True,
-                    stop=True,
-                )
-
-        keep_warm(WARM_PASSES)
+        nc.vector.memset(w_words[:, 0, :].bitcast(I32), 0)
+        nc.gpsimd.memset(w_scales[:, 0, :].bitcast(I32), 0)
+        warm_ps = psum.tile([P, OUTCH], F32, tag="bank")
+        for i in range(WARM_PASSES):
+            nc.tensor.matmul_mx(
+                out=warm_ps[:],
+                lhsT=h_codes[:, TILES - 1, warm_rows].bitcast(FP8X4),
+                lhsT_scale=h_scales[:, TILES - 1, warm_rows],
+                rhs=w_words[:, 0, :].bitcast(FP4X4),
+                rhs_scale=w_scales[:, 0, :],
+                start=True,
+                stop=True,
+            )
+        nc.vector.memset(w_scales[:, 1:PASSES, :].bitcast(I32), 0)
         gelu_seed = keep.tile([P, 1], F32)
         nc.vector.memset(gelu_seed[:], 0.0)
         ident_f32 = keep.tile([P, P], F32)
         bias_rows = keep.tile([P, BATCHES, OUTCH], BF16)
         nc.gpsimd.memset(bias_rows[:], 0.0)
-        nc.scalar.dma_start(out=bias_rows[0:1, :, :], in_=b.rearrange("b x y o -> (x y) b o"))
-        nc.scalar.dma_start(
-            out=bias_rows[1:2, :, :],
-            in_=b_out.rearrange("(x y o) -> x y o", x=1, y=1).to_broadcast([1, BATCHES, OUTCH]),
-        )
         make_identity(nc, ident_f32[:])
         ones = keep.tile([P, P], BF16)
         nc.vector.memset(ones[:], 1.0)
@@ -102,21 +91,30 @@ def tile_loratacmlp4_pb_s_kernel(tc, h, z, u, b, W_out_words, W_out_scales, b_ou
 
         h_sb = []
 
-        def load_h(j, pieces=1):
-            h_tile = h_pool.tile([P, INCH], BF16)
+        def load_h(tiles, pieces=1):
+            h_tile = h_pool.tile([P, len(tiles), INCH], BF16)
             width = INCH // pieces
             for i in range(pieces):
                 cols = slice(i * width, (i + 1) * width)
-                nc.sync.dma_start(out=h_tile[:, cols], in_=h_tiles[j][:, cols])
-            h_sb.append(h_tile)
+                nc.sync.dma_start(
+                    out=h_tile[:, :, cols],
+                    in_=h_tiles[tiles[0] : tiles[-1] + 1, :, cols].rearrange("j f i -> f j i"),
+                )
+            h_sb.extend([h_tile[:, i, :] for i in range(len(tiles))])
 
-        load_h(0, pieces=PASSES)
-        for j in range(1, EARLY_TILES):
-            load_h(j)
+        load_h((0,), pieces=PASSES)
+        load_h((1,))
         z_slots = load_factor(z_folded)
         u_slots = load_factor(u_folded)
-        for j in range(EARLY_TILES, W_BEHIND_TILES):
-            load_h(j)
+        load_h((2,))
+        load_h((3,))
+        nc.sync.dma_start(out=bias_rows[0:1, :, :], in_=b.rearrange("b x y o -> (x y) b o"))
+        nc.sync.dma_start(
+            out=bias_rows[1:2, :, :],
+            in_=b_out.rearrange("(x y o) -> x y o", x=1, y=1).to_broadcast([1, BATCHES, OUTCH]),
+        )
+        load_h((4, 5))
+
         zT_sb = keep.tile([P, TILES * ROWS], BF16)
         uT_sb = keep.tile([P, TILES * OUTCH], BF16)
         addend = keep.tile([P, TILES, OUTCH], F32)
@@ -167,7 +165,7 @@ def tile_loratacmlp4_pb_s_kernel(tc, h, z, u, b, W_out_words, W_out_scales, b_ou
             )
 
         def transpose_h(j):
-            h_words = h_sb[j][:].bitcast(F32)
+            h_words = h_sb[j].bitcast(F32)
             hT_ps = psum.tile([P, PAIRS, PASSES, ROWS], F32, tag="bank")
             for g in range(PASSES):
                 for w in range(PAIRS):
@@ -232,7 +230,6 @@ def tile_loratacmlp4_pb_s_kernel(tc, h, z, u, b, W_out_words, W_out_scales, b_ou
 
         prepare_h(0)
         prepare_h(1)
-        keep_warm(WARM_AGAIN_PASSES)
         nc.sync.dma_start(
             out=w_words[:].bitcast(I32), in_=W_out_words.rearrange("g p c -> p g c").bitcast(I32)
         )
@@ -241,17 +238,19 @@ def tile_loratacmlp4_pb_s_kernel(tc, h, z, u, b, W_out_words, W_out_scales, b_ou
                 out=w_scales[32 * q : 32 * q + 4, :, :].bitcast(I32),
                 in_=W_out_scales[:, 4 * q : 4 * q + 4, :].rearrange("g r n -> r g n").bitcast(I32),
             )
-        for j in range(W_BEHIND_TILES, TILES):
-            load_h(j)
+        load_h((6,))
+        load_h((7,))
         transpose_factor(z_slots, zT_sb, nc.scalar.copy)
         transpose_factor(u_slots, uT_sb, nc.vector.tensor_copy)
         prepare_h(2)
-        prepare_h(3)
+        grouped_3 = regroup_h(transpose_h(3))
         spread_bias()
         low_rank_addend(0)
+        quantise_h(3, grouped_3)
         prepare_h(4)
-        prepare_h(5)
+        grouped_5 = regroup_h(transpose_h(5))
         low_rank_addend(1)
+        quantise_h(5, grouped_5)
         prepare_h(6)
         grouped_last = regroup_h(transpose_h(7), pieces=PASSES)
         total_01 = add_up((0, 1), multiply((0, 1)))

import concourse.mybir as mybir
from concourse.masks import make_identity

F32 = mybir.dt.float32
BF16 = mybir.dt.bfloat16
I32 = mybir.dt.int32
U32 = mybir.dt.uint32
U8 = mybir.dt.uint8
FP8X4 = mybir.dt.float8_e4m3fn_x4
FP4X4 = mybir.dt.float4_e2m1fn_x4
ADD = mybir.AluOpType.add
MULT = mybir.AluOpType.mult
GELU = mybir.ActivationFunctionType.Gelu

P = 128
BATCHES = 2
MEMBERS = 4
TILES = BATCHES * MEMBERS
ROWS = 128
INCH = 1024
OUTCH = 128
RANK = 128
PACK = 4
K_PASS = P * PACK
PASSES = INCH // K_PASS
PAIRS = PACK // 2
WORDS_PASS = K_PASS // 2
QUADRANTS = 4
FOLD = TILES * ROWS // P
PSUM_BANKS = 8
ENDS = 5
WARM_PASSES = 14

FLOPS = 2 * TILES * ROWS * OUTCH * (INCH + RANK)


def tile_loratacmlp4_pb_s_kernel(tc, h, z, u, b, W_out_words, W_out_scales, b_out, out):
    nc = tc.nc
    h_tiles = h.rearrange("b k f i -> (b k) f i")
    z_folded = z.rearrange("b k f r -> (b k f) r").rearrange("(p s) r -> p s r", s=FOLD)
    u_folded = u.rearrange("b k o r -> (b k o) r").rearrange("(p s) r -> p s r", s=FOLD)
    out_rows = out.rearrange("b k f o -> f (b k) o")

    with (
        tc.tile_pool(name="keep", bufs=1) as keep,
        tc.tile_pool(name="h_pool", bufs=TILES) as h_pool,
        tc.tile_pool(name="factor_pool", bufs=2) as factor_pool,
        tc.tile_pool(name="work", bufs=4) as work,
        tc.tile_pool(name="ends", bufs=ENDS) as ends,
        tc.psum_pool(name="psum", bufs=PSUM_BANKS) as psum,
        tc.manual_schedule(),
    ):
        w_words = keep.tile([P, PASSES, 2 * OUTCH], U8, align_bytes=64)
        w_scales = keep.tile([P, PASSES, OUTCH], U8, align_bytes=64)
        h_codes = keep.tile([P, TILES, PASSES * ROWS], U32, align_bytes=64)
        h_scales = keep.tile([P, TILES, PASSES * ROWS], U8, align_bytes=64)
        warm_rows = slice(0, ROWS)
        nc.vector.memset(h_codes[:, TILES - 1, warm_rows], 0)
        nc.gpsimd.memset(h_scales[:, TILES - 1, warm_rows].bitcast(I32), 0)
        nc.vector.memset(w_words[:, 0, :].bitcast(I32), 0)
        nc.gpsimd.memset(w_scales[:, 0, :].bitcast(I32), 0)
        warm_ps = psum.tile([P, OUTCH], F32, tag="bank")
        for i in range(WARM_PASSES):
            nc.tensor.matmul_mx(
                out=warm_ps[:],
                lhsT=h_codes[:, TILES - 1, warm_rows].bitcast(FP8X4),
                lhsT_scale=h_scales[:, TILES - 1, warm_rows],
                rhs=w_words[:, 0, :].bitcast(FP4X4),
                rhs_scale=w_scales[:, 0, :],
                start=True,
                stop=True,
            )
        nc.vector.memset(w_scales[:, 1:PASSES, :].bitcast(I32), 0)
        gelu_seed = keep.tile([P, 1], F32)
        nc.vector.memset(gelu_seed[:], 0.0)
        ident_f32 = keep.tile([P, P], F32)
        bias_rows = keep.tile([P, BATCHES, OUTCH], BF16)
        nc.gpsimd.memset(bias_rows[:], 0.0)
        make_identity(nc, ident_f32[:])
        ones = keep.tile([P, P], BF16)
        nc.vector.memset(ones[:], 1.0)
        ident_bf16 = keep.tile([P, P], BF16)
        nc.vector.tensor_copy(out=ident_bf16[:], in_=ident_f32[:])
        gelu_warm = keep.tile([P, 1], F32)
        nc.scalar.activation(out=gelu_warm[:], in_=gelu_seed[:], func=GELU)

        def load_factor(folded):
            factor_tile = factor_pool.tile([P, FOLD, RANK], BF16)
            nc.sync.dma_start(out=factor_tile[:], in_=folded)
            return [factor_tile[:, s, :] for s in range(FOLD)]

        h_sb = []

        def load_h(tiles, pieces=1):
            h_tile = h_pool.tile([P, len(tiles), INCH], BF16)
            width = INCH // pieces
            for i in range(pieces):
                cols = slice(i * width, (i + 1) * width)
                nc.sync.dma_start(
                    out=h_tile[:, :, cols],
                    in_=h_tiles[tiles[0] : tiles[-1] + 1, :, cols].rearrange("j f i -> f j i"),
                )
            h_sb.extend([h_tile[:, i, :] for i in range(len(tiles))])

        load_h((0,), pieces=PASSES)
        load_h((1,))
        z_slots = load_factor(z_folded)
        u_slots = load_factor(u_folded)
        load_h((2,))
        load_h((3,))
        nc.sync.dma_start(out=bias_rows[0:1, :, :], in_=b.rearrange("b x y o -> (x y) b o"))
        nc.sync.dma_start(
            out=bias_rows[1:2, :, :],
            in_=b_out.rearrange("(x y o) -> x y o", x=1, y=1).to_broadcast([1, BATCHES, OUTCH]),
        )
        load_h((4, 5))

        zT_sb = keep.tile([P, TILES * ROWS], BF16)
        uT_sb = keep.tile([P, TILES * OUTCH], BF16)
        addend = keep.tile([P, TILES, OUTCH], F32)

        def transpose_factor(factor_slots, factorT_sb, copy):
            factorT_ps = psum.tile([P, FOLD, P], BF16, tag="bank")
            for s in range(FOLD):
                nc.tensor.transpose(factorT_ps[:, s, :], factor_slots[s], ident_bf16[:])
            half = P // BATCHES
            for batch in range(BATCHES):
                cols = slice(batch * half, (batch + 1) * half)
                copy(
                    out=factorT_sb[:].rearrange("r (p s) -> r p s", s=FOLD)[:, cols, :],
                    in_=factorT_ps[:].rearrange("r s p -> r p s")[:, cols, :],
                )

        bias_sb = keep.tile([P, BATCHES, OUTCH], F32)

        def spread_bias():
            bias_ps = psum.tile([P, BATCHES, OUTCH], F32, tag="bank")
            nc.tensor.matmul(
                out=bias_ps[:].rearrange("p b o -> p (b o)"),
                lhsT=ones[:],
                rhs=bias_rows[:].rearrange("p b o -> p (b o)"),
                start=True,
                stop=True,
            )
            nc.vector.tensor_copy(out=bias_sb[:], in_=bias_ps[:])

        def low_rank_addend(batch):
            lora_ps = psum.tile([P, MEMBERS, OUTCH], F32, tag="bank")
            for k in range(MEMBERS):
                j = batch * MEMBERS + k
                nc.tensor.matmul(
                    out=lora_ps[:, k, :],
                    lhsT=zT_sb[:, j * ROWS : (j + 1) * ROWS],
                    rhs=uT_sb[:, j * OUTCH : (j + 1) * OUTCH],
                    start=True,
                    stop=True,
                )
            nc.vector.scalar_tensor_tensor(
                out=addend[:, batch * MEMBERS : (batch + 1) * MEMBERS, :],
                in0=lora_ps[:],
                scalar=1.0 / RANK,
                in1=bias_sb[:, batch, :].unsqueeze(1).to_broadcast([P, MEMBERS, OUTCH]),
                op0=MULT,
                op1=ADD,
            )

        def transpose_h(j):
            h_words = h_sb[j].bitcast(F32)
            hT_ps = psum.tile([P, PAIRS, PASSES, ROWS], F32, tag="bank")
            for g in range(PASSES):
                for w in range(PAIRS):
                    nc.tensor.transpose(
                        hT_ps[:, w, g, :],
                        h_words[:, g * WORDS_PASS + w : (g + 1) * WORDS_PASS : PAIRS],
                        ident_f32[:],
                    )
            return hT_ps

        def regroup_h(hT_ps, pieces=1):
            grouped = work.tile([P, PASSES, ROWS, PACK], BF16, align_bytes=64)
            for i in range(pieces):
                gs = slice(i * PASSES // pieces, (i + 1) * PASSES // pieces)
                nc.scalar.copy(
                    out=grouped[:, gs].bitcast(F32).rearrange("p g (c i) w -> p (g c) w i", i=2),
                    in_=hT_ps[:, :, gs].rearrange("p w g (c i) -> p (g c) w i", i=2),
                )
            return grouped

        def quantise_h(j, grouped, pieces=1):
            width = PASSES * ROWS // pieces
            words = grouped[:].rearrange("p g f t -> p (g f t)")
            for i in range(pieces):
                cols = slice(i * width, (i + 1) * width)
                nc.vector.quantize_mx(
                    out=h_codes[:, j, cols].bitcast(FP8X4),
                    scales=h_scales[:, j, cols],
                    in_=words[:, PACK * i * width : PACK * (i + 1) * width],
                )

        def multiply(tiles):
            main_ps = psum.tile([P, len(tiles), OUTCH], F32, tag="bank")
            for i, j in enumerate(tiles):
                for g in range(PASSES):
                    rows = slice(g * ROWS, (g + 1) * ROWS)
                    nc.tensor.matmul_mx(
                        out=main_ps[:, i, :],
                        lhsT=h_codes[:, j, rows].bitcast(FP8X4),
                        lhsT_scale=h_scales[:, j, rows],
                        rhs=w_words[:, g, :].bitcast(FP4X4),
                        rhs_scale=w_scales[:, g, :],
                        start=(g == 0),
                        stop=(g == PASSES - 1),
                    )
            return main_ps

        def add_up(tiles, main_ps):
            total = ends.tile([P, len(tiles), OUTCH], F32)
            nc.vector.tensor_tensor(
                out=total[:], in0=main_ps[:], in1=addend[:, tiles[0] : tiles[-1] + 1, :], op=ADD
            )
            return total

        def gelu_and_store(tiles, total):
            result = ends.tile([P, len(tiles), OUTCH], F32)
            nc.scalar.activation(out=result[:], in_=total[:], func=GELU)
            nc.sync.dma_start(out=out_rows[:, tiles[0] : tiles[-1] + 1, :], in_=result[:])

        def prepare_h(j):
            quantise_h(j, regroup_h(transpose_h(j)))

        prepare_h(0)
        prepare_h(1)
        nc.sync.dma_start(
            out=w_words[:].bitcast(I32), in_=W_out_words.rearrange("g p c -> p g c").bitcast(I32)
        )
        for q in range(QUADRANTS):
            nc.sync.dma_start(
                out=w_scales[32 * q : 32 * q + 4, :, :].bitcast(I32),
                in_=W_out_scales[:, 4 * q : 4 * q + 4, :].rearrange("g r n -> r g n").bitcast(I32),
            )
        load_h((6,))
        load_h((7,))
        transpose_factor(z_slots, zT_sb, nc.scalar.copy)
        transpose_factor(u_slots, uT_sb, nc.vector.tensor_copy)
        prepare_h(2)
        grouped_3 = regroup_h(transpose_h(3))
        spread_bias()
        low_rank_addend(0)
        quantise_h(3, grouped_3)
        prepare_h(4)
        grouped_5 = regroup_h(transpose_h(5))
        low_rank_addend(1)
        quantise_h(5, grouped_5)
        prepare_h(6)
        grouped_last = regroup_h(transpose_h(7), pieces=PASSES)
        total_01 = add_up((0, 1), multiply((0, 1)))
        gelu_and_store((0, 1), total_01)
        main_23 = multiply((2, 3))
        quantise_h(7, grouped_last, pieces=PASSES)
        gelu_and_store((2, 3), add_up((2, 3), main_23))
        gelu_and_store((4, 5), add_up((4, 5), multiply((4, 5))))
        gelu_and_store((6,), add_up((6,), multiply((6,))))
        gelu_and_store((7,), add_up((7,), multiply((7,))))
